import numpy as np
import ml_dtypes


def mxq(x, axis, fmt="e4m3"):
    dtype, down = {"e4m3": (ml_dtypes.float8_e4m3fn, 7), "e5m2": (ml_dtypes.float8_e5m2, 14)}[fmt]
    v = np.moveaxis(np.asarray(x, np.float32).astype(ml_dtypes.bfloat16).astype(np.float64), axis, -1)
    blocks = v.reshape(v.shape[:-1] + (-1, 32))
    amax = np.abs(blocks).max(-1, keepdims=True)
    byte = np.maximum(np.where(amax > 0, np.frexp(amax)[1] - 1 + 127, 0) - down, 1)
    scale = np.exp2(byte - 127.0)
    codes = (blocks / scale).astype(np.float32).astype(dtype).astype(np.float64)
    return np.moveaxis((codes * scale).reshape(v.shape), -1, axis)


WIDE = False


def mx_kscale(k):
    if not WIDE:
        return np.ones(k)
    levels = np.array([20, -20, 10, -10, 0])
    a = np.random.permutation(np.resize(levels, k // 512 * 4)).reshape(k // 512, 4)
    idx = np.arange(k)
    return np.exp2(a[idx // 512, idx % 128 // 32])


BF16 = ml_dtypes.bfloat16


def bf(x):
    return np.asarray(x, np.float32).astype(BF16)


def f64(x):
    return np.asarray(x).astype(np.float64)


B, T, D, E, H, L = 128, 10, 1024, 128, 128, 2
TM = T - L
F = H + L * D + 1
K = B * TM


def setup_inputs():
    s = mx_kscale(K)[::TM]
    we = np.random.standard_normal((D, H)) / np.sqrt(H)
    wy = np.random.standard_normal((D, L, D)) * 0.7 / np.sqrt(L * D)
    wx = np.random.standard_normal((D, 1)) * 0.5
    x = np.random.standard_normal((B, T, D)) * s[:, None, None]
    emb = np.random.standard_normal((B, H)) * 0.5 * s[:, None]
    bg = np.random.standard_normal(D) * 0.3
    g = np.random.standard_normal((B, TM, D)) * np.exp2(np.random.randint(-12, 1, (B, TM, 1))) / s[:, None, None]
    return {"x": bf(x),
            "emb": bf(emb),
            "Wg": bf(np.concatenate([we, wy.reshape(D, L * D), wx], axis=1)),
            "bg": bf(bg),
            "grad_out": bf(g)}


def reference(x, emb, Wg, bg, grad_out):
    xf = f64(x)
    g = f64(grad_out)
    gq = mxq(g.reshape(K, D), 0, "e5m2")
    dWy = [(gq.T @ mxq(xf[:, l:l + TM, :].reshape(K, D), 0, "e4m3")) for l in range(L)]
    dWe = g.sum(axis=1).T @ f64(emb)
    dwx = (g * xf[:, L:, :]).sum(axis=(0, 1))[:, None]
    return np.concatenate([dWe] + dWy + [dwx], axis=1)

@@ -1,0 +1,224 @@
+from contextlib import ExitStack
+
+import concourse.mybir as mybir
+from concourse.masks import make_identity
+
+BF16 = mybir.dt.bfloat16
+F32 = mybir.dt.float32
+U32 = mybir.dt.uint32
+U8 = mybir.dt.uint8
+E4M3X4 = mybir.dt.float8_e4m3fn_x4
+E5M2X4 = mybir.dt.float8_e5m2_x4
+
+P = 128
+B, T, D, H, L = 128, 10, 1024, 128, 2
+TM = T - L
+F = H + L * D + 1
+PACK = 4
+PASSES = B * TM // (P * PACK)
+SERIES = B // PASSES
+PARTS = P // SERIES
+STEPS = PACK + L
+HALF = 512
+HALVES = D // HALF
+M_TILES = D // P
+M_PER_HALF = HALF // P
+RUN = 4
+F_PAD = 2184
+QUANTISE_LAG = 2
+GROUPED_BUFS = 4
+
+FLOPS = 2 * B * TM * D * L * D + B * TM * D + 2 * B * D * H + 2 * B * TM * D
+BYTES = 2 * (B * T * D + B * H + B * TM * D) + 4 * D * F
+
+
+def tile_npchangetransitionprior_pa_kernel(tc, x, emb, Wg, bg, grad_out, out):
+    nc = tc.nc
+    mult = mybir.AluOpType.mult
+    add = mybir.AluOpType.add
+
+    with ExitStack() as ctx:
+        keep = ctx.enter_context(tc.tile_pool(name="keep", bufs=1))
+        stage = ctx.enter_context(tc.tile_pool(name="stage", bufs=GROUPED_BUFS))
+        work = ctx.enter_context(tc.tile_pool(name="work", bufs=2))
+        lag_banks = ctx.enter_context(tc.psum_pool(name="lag_banks", bufs=4))
+        side_banks = ctx.enter_context(tc.psum_pool(name="side_banks", bufs=2))
+
+        g_raw = [keep.tile([P, PASSES, PACK, HALF], BF16, name="g_raw%d" % half) for half in range(HALVES)]
+        x_raw = [keep.tile([P, PASSES, STEPS, HALF], BF16, name="x_raw%d" % half) for half in range(HALVES)]
+        emb_raw = keep.tile([P, PASSES, H], BF16)
+        g_codes = keep.tile([P, PASSES, D], U32, align_bytes=64)
+        g_scales = keep.tile([P, PASSES, D], U8, align_bytes=64)
+        x_codes = keep.tile([P, L, PASSES, D], U32, align_bytes=64)
+        x_scales = keep.tile([P, L, PASSES, D], U8, align_bytes=64)
+        g_sum = [keep.tile([P, PASSES, HALF], F32, name="g_sum%d" % half) for half in range(HALVES)]
+        emb_f32 = keep.tile([P, PASSES, H], F32)
+        identity = keep.tile([P, P], F32)
+        out_rows = keep.tile([P, M_TILES, F_PAD], F32)
+        we_rows = keep.tile([P, M_TILES, H], F32)
+        dwx = keep.tile([P, M_TILES], F32)
+
+        g_tokens = grad_out.rearrange("b t d -> (b t) d").rearrange(
+            "(c p j) d -> c p j d", c=PASSES, p=P, j=PACK
+        )
+
+        def columns(half):
+            return slice(half * HALF, (half + 1) * HALF)
+
+        def load_half(half):
+            cols = columns(half)
+            for c in range(PASSES):
+                nc.sync.dma_start(out=g_raw[half][:, c, :, :], in_=g_tokens[c, :, :, cols])
+            for c in range(PASSES):
+                for part in range(PARTS):
+                    nc.sync.dma_start(
+                        out=x_raw[half][part:P:PARTS, c, :, :],
+                        in_=x[c * SERIES : (c + 1) * SERIES, part * PACK : part * PACK + STEPS, cols],
+                    )
+
+        def g_unit(c, half):
+            cols = columns(half)
+            return (g_raw[half][:, c, :, :], g_codes[:, c, cols], g_scales[:, c, cols], E5M2X4)
+
+        def x_unit(lag, c, half):
+            cols = columns(half)
+            return (
+                x_raw[half][:, c, lag : lag + PACK, :],
+                x_codes[:, lag, c, cols],
+                x_scales[:, lag, c, cols],
+                E4M3X4,
+            )
+
+        def prepare(units, copies):
+            grouped_tiles = []
+            for n in range(len(units) + QUANTISE_LAG):
+                if n < len(units):
+                    grouped = stage.tile([P, HALF, PACK], BF16, align_bytes=64)
+                    copies[n % len(copies)](
+                        out=grouped[:].rearrange("p (w i) j -> p w j i", i=RUN),
+                        in_=units[n][0].rearrange("p j (w i) -> p w j i", i=RUN),
+                    )
+                    grouped_tiles.append(grouped)
+                if n >= QUANTISE_LAG:
+                    codes, scales, fmt = units[n - QUANTISE_LAG][1:]
+                    nc.vector.quantize_mx(
+                        out=codes.bitcast(fmt),
+                        scales=scales,
+                        in_=grouped_tiles[n - QUANTISE_LAG][:].rearrange("p w j -> p (w j)"),
+                    )
+
+        def lag_block(m_tiles, lag, half, drains):
+            cols = columns(half)
+            first = H + lag * D + half * HALF
+            last = first + HALF
+            for m in m_tiles:
+                d_cols = slice(m * P, (m + 1) * P)
+                acc = lag_banks.tile([P, HALF], F32)
+                for c in range(PASSES):
+                    nc.tensor.matmul_mx(
+                        out=acc[:],
+                        lhsT=g_codes[:, c, d_cols].bitcast(E5M2X4),
+                        lhsT_scale=g_scales[:, c, d_cols],
+                        rhs=x_codes[:, lag, c, cols].bitcast(E4M3X4),
+                        rhs_scale=x_scales[:, lag, c, cols],
+                        start=(c == 0),
+                        stop=(c == PASSES - 1),
+                    )
+                drains[m % len(drains)](out=out_rows[:, m, first:last], in_=acc[:])
+                end = last
+                if last == F - 1:
+                    end = F
+                    drains[m % len(drains)](out=out_rows[:, m, last:F], in_=dwx[:, m : m + 1])
+                nc.sync.dma_start(out=out[d_cols, first:end], in_=out_rows[:, m, first:end])
+
+        def own_latent_products(half):
+            diag = side_banks.tile([P, M_PER_HALF, P], F32)
+            for i in range(M_PER_HALF):
+                d_cols = slice(i * P, (i + 1) * P)
+                for c in range(PASSES):
+                    for j in range(PACK):
+                        nc.tensor.matmul(
+                            out=diag[:, i, :],
+                            lhsT=g_raw[half][:, c, j, d_cols],
+                            rhs=x_raw[half][:, c, j + L, d_cols],
+                            start=(c == 0 and j == 0),
+                            stop=(c == PASSES - 1 and j == PACK - 1),
+                        )
+            return diag
+
+        def keep_diagonals(half, diag):
+            masked = work.tile([P, M_PER_HALF, P], F32)
+            nc.vector.tensor_tensor(
+                out=masked[:],
+                in0=diag[:],
+                in1=identity[:].unsqueeze(1).to_broadcast([P, M_PER_HALF, P]),
+                op=mult,
+            )
+            m_slots = slice(half * M_PER_HALF, (half + 1) * M_PER_HALF)
+            nc.vector.tensor_reduce(out=dwx[:, m_slots], in_=masked[:], axis=mybir.AxisListType.X, op=add)
+
+        def sum_tokens(half):
+            pair_sum = work.tile([P, PASSES, 2, HALF], F32)
+            nc.vector.tensor_tensor(
+                out=pair_sum[:], in0=g_raw[half][:, :, 0:2, :], in1=g_raw[half][:, :, 2:4, :], op=add
+            )
+            nc.vector.tensor_tensor(
+                out=g_sum[half][:], in0=pair_sum[:, :, 0, :], in1=pair_sum[:, :, 1, :], op=add
+            )
+
+        def emb_block(half):
+            d_we = side_banks.tile([P, M_PER_HALF, H], F32)
+            for i in range(M_PER_HALF):
+                for c in range(PASSES):
+                    nc.tensor.matmul(
+                        out=d_we[:, i, :],
+                        lhsT=g_sum[half][:, c, i * P : (i + 1) * P],
+                        rhs=emb_f32[:, c, :],
+                        start=(c == 0),
+                        stop=(c == PASSES - 1),
+                    )
+            m_slots = slice(half * M_PER_HALF, (half + 1) * M_PER_HALF)
+            nc.scalar.copy(out=we_rows[:, m_slots, :], in_=d_we[:])
+            nc.sync.dma_start(
+                out=out[half * HALF : (half + 1) * HALF, 0:H].rearrange("(m p) h -> p m h", p=P),
+                in_=we_rows[:, m_slots, :],
+            )
+
+        make_identity(nc, identity[:])
+        for c in range(PASSES):
+            for part in range(PARTS):
+                nc.scalar.dma_start(
+                    out=emb_raw[part:P:PARTS, c, :], in_=emb[c * SERIES : (c + 1) * SERIES, :]
+                )
+        for half in range(HALVES):
+            load_half(half)
+
+        left = range(M_PER_HALF)
+        right = range(M_PER_HALF, M_TILES)
+        both = [nc.vector.tensor_copy, nc.scalar.copy]
+        vector_only = [nc.vector.tensor_copy]
+
+        scalar_only = [nc.scalar.copy]
+
+        prepare(
+            [g_unit(c, 0) for c in range(PASSES)]
+            + [x_unit(lag, c, 0) for lag in range(L) for c in range(PASSES)],
+            both,
+        )
+        diag_left = own_latent_products(0)
+        for lag in range(L):
+            lag_block(left, lag, 0, scalar_only)
+        prepare([g_unit(c, 1) for c in range(PASSES)], vector_only)
+        for lag in range(L):
+            lag_block(right, lag, 0, scalar_only)
+        prepare([x_unit(lag, c, 1) for lag in range(L) for c in range(PASSES)], vector_only)
+        keep_diagonals(0, diag_left)
+        nc.vector.tensor_copy(out=emb_f32[:], in_=emb_raw[:])
+        for half in range(HALVES):
+            sum_tokens(half)
+        lag_block(range(M_TILES), 0, 1, scalar_only)
+        diag_right = own_latent_products(1)
+        keep_diagonals(1, diag_right)
+        for half in range(HALVES):
+            emb_block(half)
+        lag_block(range(M_TILES), 1, 1, both)

@@ -43,6 +43,7 @@ def tile_npchangetransitionprior_pa_kernel(tc, x, emb, Wg, bg, grad_out, out):
         work = ctx.enter_context(tc.tile_pool(name="work", bufs=2))
         lag_banks = ctx.enter_context(tc.psum_pool(name="lag_banks", bufs=4))
         side_banks = ctx.enter_context(tc.psum_pool(name="side_banks", bufs=2))
+        ctx.enter_context(tc.manual_schedule())
 
         g_raw = [keep.tile([P, PASSES, PACK, HALF], BF16, name="g_raw%d" % half) for half in range(HALVES)]
         x_raw = [keep.tile([P, PASSES, STEPS, HALF], BF16, name="x_raw%d" % half) for half in range(HALVES)]
@@ -89,15 +90,16 @@ def tile_npchangetransitionprior_pa_kernel(tc, x, emb, Wg, bg, grad_out, out):
                 E4M3X4,
             )
 
-        def prepare(units, copies):
+        def prepare(units, shares):
             grouped_tiles = []
             for n in range(len(units) + QUANTISE_LAG):
                 if n < len(units):
                     grouped = stage.tile([P, HALF, PACK], BF16, align_bytes=64)
-                    copies[n % len(copies)](
-                        out=grouped[:].rearrange("p (w i) j -> p w j i", i=RUN),
-                        in_=units[n][0].rearrange("p j (w i) -> p w j i", i=RUN),
-                    )
+                    for copy, share in shares:
+                        copy(
+                            out=grouped[:, share, :].rearrange("p (w i) j -> p w j i", i=RUN),
+                            in_=units[n][0][:, :, share].rearrange("p j (w i) -> p w j i", i=RUN),
+                        )
                     grouped_tiles.append(grouped)
                 if n >= QUANTISE_LAG:
                     codes, scales, fmt = units[n - QUANTISE_LAG][1:]
@@ -195,30 +197,31 @@ def tile_npchangetransitionprior_pa_kernel(tc, x, emb, Wg, bg, grad_out, out):
 
         left = range(M_PER_HALF)
         right = range(M_PER_HALF, M_TILES)
-        both = [nc.vector.tensor_copy, nc.scalar.copy]
-        vector_only = [nc.vector.tensor_copy]
-
-        scalar_only = [nc.scalar.copy]
+        shared = [(nc.vector.tensor_copy, slice(0, HALF // 2)), (nc.scalar.copy, slice(HALF // 2, HALF))]
+        vector_only = [(nc.vector.tensor_copy, slice(0, HALF))]
+        scalar_drains = [nc.scalar.copy]
+        both_drain = [nc.scalar.copy, nc.vector.tensor_copy]
 
         prepare(
             [g_unit(c, 0) for c in range(PASSES)]
             + [x_unit(lag, c, 0) for lag in range(L) for c in range(PASSES)],
-            both,
+            shared,
         )
         diag_left = own_latent_products(0)
         for lag in range(L):
-            lag_block(left, lag, 0, scalar_only)
+            lag_block(left, lag, 0, scalar_drains)
         prepare([g_unit(c, 1) for c in range(PASSES)], vector_only)
+        diag_right = own_latent_products(1)
         for lag in range(L):
-            lag_block(right, lag, 0, scalar_only)
+            lag_block(right, lag, 0, scalar_drains)
         prepare([x_unit(lag, c, 1) for lag in range(L) for c in range(PASSES)], vector_only)
         keep_diagonals(0, diag_left)
         nc.vector.tensor_copy(out=emb_f32[:], in_=emb_raw[:])
         for half in range(HALVES):
             sum_tokens(half)
-        lag_block(range(M_TILES), 0, 1, scalar_only)
-        diag_right = own_latent_products(1)
         keep_diagonals(1, diag_right)
+        lag_block(range(M_TILES), 0, 1, scalar_drains)
+        lag_block(left, 1, 1, scalar_drains)
         for half in range(HALVES):
             emb_block(half)
-        lag_block(range(M_TILES), 1, 1, both)
+        lag_block(right, 1, 1, both_drain)

@@ -24,7 +24,7 @@ HALVES = D // HALF
 M_TILES = D // P
 M_PER_HALF = HALF // P
 RUN = 4
-F_PAD = 2184
+ROW_PAD = 2056
 QUANTISE_LAG = 2
 GROUPED_BUFS = 4
 
@@ -46,7 +46,7 @@ def tile_npchangetransitionprior_pa_kernel(tc, x, emb, Wg, bg, grad_out, out):
         ctx.enter_context(tc.manual_schedule())
 
         g_raw = [keep.tile([P, PASSES, PACK, HALF], BF16, name="g_raw%d" % half) for half in range(HALVES)]
-        x_raw = [keep.tile([P, PASSES, STEPS, HALF], BF16, name="x_raw%d" % half) for half in range(HALVES)]
+        x_raw = [keep.tile([P, STEPS, D], BF16, name="x_raw%d" % c) for c in range(PASSES)]
         emb_raw = keep.tile([P, PASSES, H], BF16)
         g_codes = keep.tile([P, PASSES, D], U32, align_bytes=64)
         g_scales = keep.tile([P, PASSES, D], U8, align_bytes=64)
@@ -55,7 +55,7 @@ def tile_npchangetransitionprior_pa_kernel(tc, x, emb, Wg, bg, grad_out, out):
         g_sum = [keep.tile([P, PASSES, HALF], F32, name="g_sum%d" % half) for half in range(HALVES)]
         emb_f32 = keep.tile([P, PASSES, H], F32)
         identity = keep.tile([P, P], F32)
-        out_rows = keep.tile([P, M_TILES, F_PAD], F32)
+        lag_rows = keep.tile([P, M_TILES, ROW_PAD], F32)
         we_rows = keep.tile([P, M_TILES, H], F32)
         dwx = keep.tile([P, M_TILES], F32)
 
@@ -66,16 +66,16 @@ def tile_npchangetransitionprior_pa_kernel(tc, x, emb, Wg, bg, grad_out, out):
         def columns(half):
             return slice(half * HALF, (half + 1) * HALF)
 
-        def load_half(half):
-            cols = columns(half)
+        def load_g(half):
             for c in range(PASSES):
-                nc.sync.dma_start(out=g_raw[half][:, c, :, :], in_=g_tokens[c, :, :, cols])
-            for c in range(PASSES):
-                for part in range(PARTS):
-                    nc.sync.dma_start(
-                        out=x_raw[half][part:P:PARTS, c, :, :],
-                        in_=x[c * SERIES : (c + 1) * SERIES, part * PACK : part * PACK + STEPS, cols],
-                    )
+                nc.sync.dma_start(out=g_raw[half][:, c, :, :], in_=g_tokens[c, :, :, columns(half)])
+
+        def load_x(c):
+            for part in range(PARTS):
+                nc.sync.dma_start(
+                    out=x_raw[c][part:P:PARTS, :, :],
+                    in_=x[c * SERIES : (c + 1) * SERIES, part * PACK : part * PACK + STEPS, :],
+                )
 
         def g_unit(c, half):
             cols = columns(half)
@@ -84,7 +84,7 @@ def tile_npchangetransitionprior_pa_kernel(tc, x, emb, Wg, bg, grad_out, out):
         def x_unit(lag, c, half):
             cols = columns(half)
             return (
-                x_raw[half][:, c, lag : lag + PACK, :],
+                x_raw[c][:, lag : lag + PACK, cols],
                 x_codes[:, lag, c, cols],
                 x_scales[:, lag, c, cols],
                 E4M3X4,
@@ -109,40 +109,40 @@ def tile_npchangetransitionprior_pa_kernel(tc, x, emb, Wg, bg, grad_out, out):
                         in_=grouped_tiles[n - QUANTISE_LAG][:].rearrange("p w j -> p (w j)"),
                     )
 
-        def lag_block(m_tiles, lag, half, drains):
-            cols = columns(half)
-            first = H + lag * D + half * HALF
-            last = first + HALF
+        def lag_block(m_tiles, lag, drains):
             for m in m_tiles:
                 d_cols = slice(m * P, (m + 1) * P)
-                acc = lag_banks.tile([P, HALF], F32)
-                for c in range(PASSES):
-                    nc.tensor.matmul_mx(
-                        out=acc[:],
-                        lhsT=g_codes[:, c, d_cols].bitcast(E5M2X4),
-                        lhsT_scale=g_scales[:, c, d_cols],
-                        rhs=x_codes[:, lag, c, cols].bitcast(E4M3X4),
-                        rhs_scale=x_scales[:, lag, c, cols],
-                        start=(c == 0),
-                        stop=(c == PASSES - 1),
-                    )
-                drains[m % len(drains)](out=out_rows[:, m, first:last], in_=acc[:])
-                end = last
-                if last == F - 1:
-                    end = F
-                    drains[m % len(drains)](out=out_rows[:, m, last:F], in_=dwx[:, m : m + 1])
-                nc.sync.dma_start(out=out[d_cols, first:end], in_=out_rows[:, m, first:end])
+                for half in range(HALVES):
+                    cols = columns(half)
+                    acc = lag_banks.tile([P, HALF], F32)
+                    for c in range(PASSES):
+                        nc.tensor.matmul_mx(
+                            out=acc[:],
+                            lhsT=g_codes[:, c, d_cols].bitcast(E5M2X4),
+                            lhsT_scale=g_scales[:, c, d_cols],
+                            rhs=x_codes[:, lag, c, cols].bitcast(E4M3X4),
+                            rhs_scale=x_scales[:, lag, c, cols],
+                            start=(c == 0),
+                            stop=(c == PASSES - 1),
+                        )
+                    first = lag * D + half * HALF
+                    drains[half % len(drains)](out=lag_rows[:, m, first : first + HALF], in_=acc[:])
+                first = lag * D
+                last = first + D
+                if lag == L - 1:
+                    drains[0](out=lag_rows[:, m, last : last + 1], in_=dwx[:, m : m + 1])
+                    last = last + 1
+                nc.sync.dma_start(out=out[d_cols, H + first : H + last], in_=lag_rows[:, m, first:last])
 
         def own_latent_products(half):
             diag = side_banks.tile([P, M_PER_HALF, P], F32)
             for i in range(M_PER_HALF):
-                d_cols = slice(i * P, (i + 1) * P)
                 for c in range(PASSES):
                     for j in range(PACK):
                         nc.tensor.matmul(
                             out=diag[:, i, :],
-                            lhsT=g_raw[half][:, c, j, d_cols],
-                            rhs=x_raw[half][:, c, j + L, d_cols],
+                            lhsT=g_raw[half][:, c, j, i * P : (i + 1) * P],
+                            rhs=x_raw[c][:, j + L, half * HALF + i * P : half * HALF + (i + 1) * P],
                             start=(c == 0 and j == 0),
                             stop=(c == PASSES - 1 and j == PACK - 1),
                         )
@@ -187,13 +187,15 @@ def tile_npchangetransitionprior_pa_kernel(tc, x, emb, Wg, bg, grad_out, out):
             )
 
         make_identity(nc, identity[:])
+        load_g(0)
+        for c in range(PASSES):
+            load_x(c)
+        load_g(1)
         for c in range(PASSES):
             for part in range(PARTS):
-                nc.scalar.dma_start(
+                nc.sync.dma_start(
                     out=emb_raw[part:P:PARTS, c, :], in_=emb[c * SERIES : (c + 1) * SERIES, :]
                 )
-        for half in range(HALVES):
-            load_half(half)
 
         left = range(M_PER_HALF)
         right = range(M_PER_HALF, M_TILES)
@@ -202,26 +204,20 @@ def tile_npchangetransitionprior_pa_kernel(tc, x, emb, Wg, bg, grad_out, out):
         scalar_drains = [nc.scalar.copy]
         both_drain = [nc.scalar.copy, nc.vector.tensor_copy]
 
-        prepare(
-            [g_unit(c, 0) for c in range(PASSES)]
-            + [x_unit(lag, c, 0) for lag in range(L) for c in range(PASSES)],
-            shared,
-        )
+        prepare([g_unit(c, 0) for c in range(PASSES)], shared)
+        sum_tokens(0)
+        prepare([x_unit(0, c, half) for c in range(PASSES) for half in range(HALVES)], shared)
         diag_left = own_latent_products(0)
-        for lag in range(L):
-            lag_block(left, lag, 0, scalar_drains)
+        lag_block(left, 0, scalar_drains)
         prepare([g_unit(c, 1) for c in range(PASSES)], vector_only)
         diag_right = own_latent_products(1)
-        for lag in range(L):
-            lag_block(right, lag, 0, scalar_drains)
-        prepare([x_unit(lag, c, 1) for lag in range(L) for c in range(PASSES)], vector_only)
+        lag_block(right, 0, scalar_drains)
+        prepare([x_unit(1, c, half) for c in range(PASSES) for half in range(HALVES)], vector_only)
         keep_diagonals(0, diag_left)
-        nc.vector.tensor_copy(out=emb_f32[:], in_=emb_raw[:])
-        for half in range(HALVES):
-            sum_tokens(half)
         keep_diagonals(1, diag_right)
-        lag_block(range(M_TILES), 0, 1, scalar_drains)
-        lag_block(left, 1, 1, scalar_drains)
+        nc.vector.tensor_copy(out=emb_f32[:], in_=emb_raw[:])
+        sum_tokens(1)
+        lag_block(left, 1, scalar_drains)
         for half in range(HALVES):
             emb_block(half)
-        lag_block(right, 1, 1, both_drain)
+        lag_block(right, 1, both_drain)

@@ -112,6 +112,11 @@ def tile_npchangetransitionprior_pa_kernel(tc, x, emb, Wg, bg, grad_out, out):
         def lag_block(m_tiles, lag, drains):
             for m in m_tiles:
                 d_cols = slice(m * P, (m + 1) * P)
+                first = lag * D
+                last = first + D
+                if lag == L - 1:
+                    drains[0](out=lag_rows[:, m, last : last + 1], in_=dwx[:, m : m + 1])
+                    last = last + 1
                 for half in range(HALVES):
                     cols = columns(half)
                     acc = lag_banks.tile([P, HALF], F32)
@@ -125,13 +130,9 @@ def tile_npchangetransitionprior_pa_kernel(tc, x, emb, Wg, bg, grad_out, out):
                             start=(c == 0),
                             stop=(c == PASSES - 1),
                         )
-                    first = lag * D + half * HALF
-                    drains[half % len(drains)](out=lag_rows[:, m, first : first + HALF], in_=acc[:])
-                first = lag * D
-                last = first + D
-                if lag == L - 1:
-                    drains[0](out=lag_rows[:, m, last : last + 1], in_=dwx[:, m : m + 1])
-                    last = last + 1
+                    drains[half % len(drains)](
+                        out=lag_rows[:, m, first + half * HALF : first + (half + 1) * HALF], in_=acc[:]
+                    )
                 nc.sync.dma_start(out=out[d_cols, H + first : H + last], in_=lag_rows[:, m, first:last])
 
         def own_latent_products(half):
@@ -160,15 +161,16 @@ def tile_npchangetransitionprior_pa_kernel(tc, x, emb, Wg, bg, grad_out, out):
             nc.vector.tensor_reduce(out=dwx[:, m_slots], in_=masked[:], axis=mybir.AxisListType.X, op=add)
 
         def sum_tokens(half):
-            pair_sum = work.tile([P, PASSES, 2, HALF], F32)
-            nc.vector.tensor_tensor(
-                out=pair_sum[:], in0=g_raw[half][:, :, 0:2, :], in1=g_raw[half][:, :, 2:4, :], op=add
-            )
-            nc.vector.tensor_tensor(
-                out=g_sum[half][:], in0=pair_sum[:, :, 0, :], in1=pair_sum[:, :, 1, :], op=add
-            )
+            for c in range(PASSES):
+                pair_sum = work.tile([P, 2, HALF], F32)
+                nc.vector.tensor_tensor(
+                    out=pair_sum[:], in0=g_raw[half][:, c, 0:2, :], in1=g_raw[half][:, c, 2:4, :], op=add
+                )
+                nc.vector.tensor_tensor(
+                    out=g_sum[half][:, c, :], in0=pair_sum[:, 0, :], in1=pair_sum[:, 1, :], op=add
+                )
 
-        def emb_block(half):
+        def emb_products(half):
             d_we = side_banks.tile([P, M_PER_HALF, H], F32)
             for i in range(M_PER_HALF):
                 for c in range(PASSES):
@@ -179,6 +181,9 @@ def tile_npchangetransitionprior_pa_kernel(tc, x, emb, Wg, bg, grad_out, out):
                         start=(c == 0),
                         stop=(c == PASSES - 1),
                     )
+            return d_we
+
+        def store_emb(half, d_we):
             m_slots = slice(half * M_PER_HALF, (half + 1) * M_PER_HALF)
             nc.scalar.copy(out=we_rows[:, m_slots, :], in_=d_we[:])
             nc.sync.dma_start(
@@ -187,15 +192,14 @@ def tile_npchangetransitionprior_pa_kernel(tc, x, emb, Wg, bg, grad_out, out):
             )
 
         make_identity(nc, identity[:])
+        for part in range(PARTS):
+            nc.scalar.dma_start(
+                out=emb_raw[part:P:PARTS, :, :], in_=emb.rearrange("(c s) h -> s c h", c=PASSES)
+            )
         load_g(0)
         for c in range(PASSES):
             load_x(c)
         load_g(1)
-        for c in range(PASSES):
-            for part in range(PARTS):
-                nc.sync.dma_start(
-                    out=emb_raw[part:P:PARTS, c, :], in_=emb[c * SERIES : (c + 1) * SERIES, :]
-                )
 
         left = range(M_PER_HALF)
         right = range(M_PER_HALF, M_TILES)
@@ -204,20 +208,23 @@ def tile_npchangetransitionprior_pa_kernel(tc, x, emb, Wg, bg, grad_out, out):
         scalar_drains = [nc.scalar.copy]
         both_drain = [nc.scalar.copy, nc.vector.tensor_copy]
 
-        prepare([g_unit(c, 0) for c in range(PASSES)], shared)
         sum_tokens(0)
-        prepare([x_unit(0, c, half) for c in range(PASSES) for half in range(HALVES)], shared)
+        nc.vector.tensor_copy(out=emb_f32[:], in_=emb_raw[:])
+        we_left = emb_products(0)
+        prepare([g_unit(c, 0) for c in range(PASSES)], shared)
+        for c in range(PASSES):
+            prepare([x_unit(0, c, half) for half in range(HALVES)], shared)
         diag_left = own_latent_products(0)
+        store_emb(0, we_left)
         lag_block(left, 0, scalar_drains)
         prepare([g_unit(c, 1) for c in range(PASSES)], vector_only)
         diag_right = own_latent_products(1)
         lag_block(right, 0, scalar_drains)
         prepare([x_unit(1, c, half) for c in range(PASSES) for half in range(HALVES)], vector_only)
         keep_diagonals(0, diag_left)
-        keep_diagonals(1, diag_right)
-        nc.vector.tensor_copy(out=emb_f32[:], in_=emb_raw[:])
         sum_tokens(1)
+        keep_diagonals(1, diag_right)
         lag_block(left, 1, scalar_drains)
-        for half in range(HALVES):
-            emb_block(half)
+        we_right = emb_products(1)
+        store_emb(1, we_right)
         lag_block(right, 1, both_drain)

@@ -25,7 +25,6 @@ M_TILES = D // P
 M_PER_HALF = HALF // P
 RUN = 4
 ROW_PAD = 2056
-QUANTISE_LAG = 2
 GROUPED_BUFS = 4
 
 FLOPS = 2 * B * TM * D * L * D + B * TM * D + 2 * B * D * H + 2 * B * TM * D
@@ -46,18 +45,21 @@ def tile_npchangetransitionprior_pa_kernel(tc, x, emb, Wg, bg, grad_out, out):
         ctx.enter_context(tc.manual_schedule())
 
         g_raw = [keep.tile([P, PASSES, PACK, HALF], BF16, name="g_raw%d" % half) for half in range(HALVES)]
-        x_raw = [keep.tile([P, STEPS, D], BF16, name="x_raw%d" % c) for c in range(PASSES)]
+        x_raw = [
+            [keep.tile([P, STEPS, HALF], BF16, name="x_raw%d_%d" % (c, half)) for half in range(HALVES)]
+            for c in range(PASSES)
+        ]
         emb_raw = keep.tile([P, PASSES, H], BF16)
         g_codes = keep.tile([P, PASSES, D], U32, align_bytes=64)
         g_scales = keep.tile([P, PASSES, D], U8, align_bytes=64)
         x_codes = keep.tile([P, L, PASSES, D], U32, align_bytes=64)
         x_scales = keep.tile([P, L, PASSES, D], U8, align_bytes=64)
-        g_sum = [keep.tile([P, PASSES, HALF], F32, name="g_sum%d" % half) for half in range(HALVES)]
+        g_sum = keep.tile([P, PASSES, HALF], F32)
         emb_f32 = keep.tile([P, PASSES, H], F32)
+        last_tokens = keep.tile([P, P], F32)
         identity = keep.tile([P, P], F32)
         lag_rows = keep.tile([P, M_TILES, ROW_PAD], F32)
         we_rows = keep.tile([P, M_TILES, H], F32)
-        dwx = keep.tile([P, M_TILES], F32)
 
         g_tokens = grad_out.rearrange("b t d -> (b t) d").rearrange(
             "(c p j) d -> c p j d", c=PASSES, p=P, j=PACK
@@ -70,12 +72,13 @@ def tile_npchangetransitionprior_pa_kernel(tc, x, emb, Wg, bg, grad_out, out):
             for c in range(PASSES):
                 nc.sync.dma_start(out=g_raw[half][:, c, :, :], in_=g_tokens[c, :, :, columns(half)])
 
-        def load_x(c):
-            for part in range(PARTS):
-                nc.sync.dma_start(
-                    out=x_raw[c][part:P:PARTS, :, :],
-                    in_=x[c * SERIES : (c + 1) * SERIES, part * PACK : part * PACK + STEPS, :],
-                )
+        def load_x(half):
+            for c in range(PASSES):
+                for part in range(PARTS):
+                    nc.sync.dma_start(
+                        out=x_raw[c][half][part:P:PARTS, :, :],
+                        in_=x[c * SERIES : (c + 1) * SERIES, part * PACK : part * PACK + STEPS, columns(half)],
+                    )
 
         def g_unit(c, half):
             cols = columns(half)
@@ -84,55 +87,50 @@ def tile_npchangetransitionprior_pa_kernel(tc, x, emb, Wg, bg, grad_out, out):
         def x_unit(lag, c, half):
             cols = columns(half)
             return (
-                x_raw[c][:, lag : lag + PACK, cols],
+                x_raw[c][half][:, lag : lag + PACK, :],
                 x_codes[:, lag, c, cols],
                 x_scales[:, lag, c, cols],
                 E4M3X4,
             )
 
-        def prepare(units, shares):
-            grouped_tiles = []
-            for n in range(len(units) + QUANTISE_LAG):
-                if n < len(units):
-                    grouped = stage.tile([P, HALF, PACK], BF16, align_bytes=64)
-                    for copy, share in shares:
-                        copy(
-                            out=grouped[:, share, :].rearrange("p (w i) j -> p w j i", i=RUN),
-                            in_=units[n][0][:, :, share].rearrange("p j (w i) -> p w j i", i=RUN),
-                        )
-                    grouped_tiles.append(grouped)
-                if n >= QUANTISE_LAG:
-                    codes, scales, fmt = units[n - QUANTISE_LAG][1:]
-                    nc.vector.quantize_mx(
-                        out=codes.bitcast(fmt),
-                        scales=scales,
-                        in_=grouped_tiles[n - QUANTISE_LAG][:].rearrange("p w j -> p (w j)"),
-                    )
+        def regroup(unit, shares):
+            grouped = stage.tile([P, HALF, PACK], BF16, align_bytes=64)
+            for copy, share in shares:
+                copy(
+                    out=grouped[:, share, :].rearrange("p (w i) j -> p w j i", i=RUN),
+                    in_=unit[0][:, :, share].rearrange("p j (w i) -> p w j i", i=RUN),
+                )
+            return grouped
 
-        def lag_block(m_tiles, lag, drains):
-            for m in m_tiles:
+        def quantise(unit, grouped):
+            codes, scales, fmt = unit[1:]
+            nc.vector.quantize_mx(
+                out=codes.bitcast(fmt), scales=scales, in_=grouped[:].rearrange("p w j -> p (w j)")
+            )
+
+        def prepare(units, shares):
+            grouped = [regroup(unit, shares) for unit in units]
+            for unit, unit_grouped in zip(units, grouped):
+                quantise(unit, unit_grouped)
+
+        def lag_block(m_tiles, lag, half, drains):
+            cols = columns(half)
+            first = lag * D + half * HALF
+            last = first + HALF + (1 if first + HALF == L * D else 0)
+            for n, m in enumerate(m_tiles):
                 d_cols = slice(m * P, (m + 1) * P)
-                first = lag * D
-                last = first + D
-                if lag == L - 1:
-                    drains[0](out=lag_rows[:, m, last : last + 1], in_=dwx[:, m : m + 1])
-                    last = last + 1
-                for half in range(HALVES):
-                    cols = columns(half)
-                    acc = lag_banks.tile([P, HALF], F32)
-                    for c in range(PASSES):
-                        nc.tensor.matmul_mx(
-                            out=acc[:],
-                            lhsT=g_codes[:, c, d_cols].bitcast(E5M2X4),
-                            lhsT_scale=g_scales[:, c, d_cols],
-                            rhs=x_codes[:, lag, c, cols].bitcast(E4M3X4),
-                            rhs_scale=x_scales[:, lag, c, cols],
-                            start=(c == 0),
-                            stop=(c == PASSES - 1),
-                        )
-                    drains[half % len(drains)](
-                        out=lag_rows[:, m, first + half * HALF : first + (half + 1) * HALF], in_=acc[:]
+                acc = lag_banks.tile([P, HALF], F32)
+                for c in range(PASSES):
+                    nc.tensor.matmul_mx(
+                        out=acc[:],
+                        lhsT=g_codes[:, c, d_cols].bitcast(E5M2X4),
+                        lhsT_scale=g_scales[:, c, d_cols],
+                        rhs=x_codes[:, lag, c, cols].bitcast(E4M3X4),
+                        rhs_scale=x_scales[:, lag, c, cols],
+                        start=(c == 0),
+                        stop=(c == PASSES - 1),
                     )
+                drains[n % len(drains)](out=lag_rows[:, m, first : first + HALF], in_=acc[:])
                 nc.sync.dma_start(out=out[d_cols, H + first : H + last], in_=lag_rows[:, m, first:last])
 
         def own_latent_products(half):
@@ -143,7 +141,7 @@ def tile_npchangetransitionprior_pa_kernel(tc, x, emb, Wg, bg, grad_out, out):
                         nc.tensor.matmul(
                             out=diag[:, i, :],
                             lhsT=g_raw[half][:, c, j, i * P : (i + 1) * P],
-                            rhs=x_raw[c][:, j + L, half * HALF + i * P : half * HALF + (i + 1) * P],
+                            rhs=x_raw[c][half][:, j + L, i * P : (i + 1) * P],
                             start=(c == 0 and j == 0),
                             stop=(c == PASSES - 1 and j == PACK - 1),
                         )
@@ -158,7 +156,39 @@ def tile_npchangetransitionprior_pa_kernel(tc, x, emb, Wg, bg, grad_out, out):
                 op=mult,
             )
             m_slots = slice(half * M_PER_HALF, (half + 1) * M_PER_HALF)
-            nc.vector.tensor_reduce(out=dwx[:, m_slots], in_=masked[:], axis=mybir.AxisListType.X, op=add)
+            nc.vector.tensor_reduce(
+                out=lag_rows[:, m_slots, L * D], in_=masked[:], axis=mybir.AxisListType.X, op=add
+            )
+
+        def add_last_tokens(half):
+            nc.vector.tensor_tensor(
+                out=last_tokens[:],
+                in0=g_raw[half][:, PASSES - 1, PACK - 2, HALF - P : HALF],
+                in1=g_raw[half][:, PASSES - 1, PACK - 1, HALF - P : HALF],
+                op=add,
+            )
+
+        def emb_products_by_token(half):
+            d_we = side_banks.tile([P, M_PER_HALF, H], F32)
+            slots = [(c, j) for c in range(PASSES) for j in range(PACK)]
+            for i in range(M_PER_HALF):
+                single = slots if i < M_PER_HALF - 1 else slots[:-2]
+                for c, j in single:
+                    nc.tensor.matmul(
+                        out=d_we[:, i, :],
+                        lhsT=g_raw[half][:, c, j, i * P : (i + 1) * P],
+                        rhs=emb_raw[:, c, :],
+                        start=((c, j) == slots[0]),
+                        stop=((c, j) == slots[-1]),
+                    )
+            nc.tensor.matmul(
+                out=d_we[:, M_PER_HALF - 1, :],
+                lhsT=last_tokens[:],
+                rhs=emb_f32[:, PASSES - 1, :],
+                start=False,
+                stop=True,
+            )
+            return d_we
 
         def sum_tokens(half):
             for c in range(PASSES):
@@ -167,16 +197,16 @@ def tile_npchangetransitionprior_pa_kernel(tc, x, emb, Wg, bg, grad_out, out):
                     out=pair_sum[:], in0=g_raw[half][:, c, 0:2, :], in1=g_raw[half][:, c, 2:4, :], op=add
                 )
                 nc.vector.tensor_tensor(
-                    out=g_sum[half][:, c, :], in0=pair_sum[:, 0, :], in1=pair_sum[:, 1, :], op=add
+                    out=g_sum[:, c, :], in0=pair_sum[:, 0, :], in1=pair_sum[:, 1, :], op=add
                 )
 
-        def emb_products(half):
+        def emb_products_of_sums():
             d_we = side_banks.tile([P, M_PER_HALF, H], F32)
             for i in range(M_PER_HALF):
                 for c in range(PASSES):
                     nc.tensor.matmul(
                         out=d_we[:, i, :],
-                        lhsT=g_sum[half][:, c, i * P : (i + 1) * P],
+                        lhsT=g_sum[:, c, i * P : (i + 1) * P],
                         rhs=emb_f32[:, c, :],
                         start=(c == 0),
                         stop=(c == PASSES - 1),
@@ -197,9 +227,9 @@ def tile_npchangetransitionprior_pa_kernel(tc, x, emb, Wg, bg, grad_out, out):
                 out=emb_raw[part:P:PARTS, :, :], in_=emb.rearrange("(c s) h -> s c h", c=PASSES)
             )
         load_g(0)
-        for c in range(PASSES):
-            load_x(c)
+        load_x(0)
         load_g(1)
+        load_x(1)
 
         left = range(M_PER_HALF)
         right = range(M_PER_HALF, M_TILES)
@@ -208,23 +238,38 @@ def tile_npchangetransitionprior_pa_kernel(tc, x, emb, Wg, bg, grad_out, out):
         scalar_drains = [nc.scalar.copy]
         both_drain = [nc.scalar.copy, nc.vector.tensor_copy]
 
-        sum_tokens(0)
+        left_units = [g_unit(c, 0) for c in range(PASSES)]
+        left_grouped = [regroup(unit, shared) for unit in left_units]
         nc.vector.tensor_copy(out=emb_f32[:], in_=emb_raw[:])
-        we_left = emb_products(0)
-        prepare([g_unit(c, 0) for c in range(PASSES)], shared)
-        for c in range(PASSES):
-            prepare([x_unit(0, c, half) for half in range(HALVES)], shared)
+        add_last_tokens(0)
+        we_left = emb_products_by_token(0)
+        for unit, unit_grouped in zip(left_units, left_grouped):
+            quantise(unit, unit_grouped)
+        first_units = [x_unit(lag, c, 0) for lag in range(L) for c in range(PASSES)]
+        grouped = [regroup(first_units[0], shared)]
+        quantise(first_units[0], grouped[0])
+        grouped.append(regroup(first_units[1], shared))
+        grouped.append(regroup(first_units[2], shared))
+        quantise(first_units[1], grouped[1])
+        grouped.append(regroup(first_units[3], shared))
+        quantise(first_units[2], grouped[2])
+        quantise(first_units[3], grouped[3])
         diag_left = own_latent_products(0)
+        lag_block(left, 0, 0, scalar_drains)
+        lag_block(left, 1, 0, scalar_drains)
         store_emb(0, we_left)
-        lag_block(left, 0, scalar_drains)
         prepare([g_unit(c, 1) for c in range(PASSES)], vector_only)
         diag_right = own_latent_products(1)
-        lag_block(right, 0, scalar_drains)
-        prepare([x_unit(1, c, half) for c in range(PASSES) for half in range(HALVES)], vector_only)
+        lag_block(right, 0, 0, scalar_drains)
+        lag_block(right, 1, 0, scalar_drains)
+        for lag in range(L):
+            prepare([x_unit(lag, c, 1) for c in range(PASSES)], vector_only)
         keep_diagonals(0, diag_left)
-        sum_tokens(1)
         keep_diagonals(1, diag_right)
-        lag_block(left, 1, scalar_drains)
-        we_right = emb_products(1)
+        lag_block(left, 0, 1, scalar_drains)
+        lag_block(right, 0, 1, scalar_drains)
+        sum_tokens(1)
+        lag_block(left, 1, 1, scalar_drains)
+        lag_block(right, 1, 1, both_drain)
+        we_right = emb_products_of_sums()
         store_emb(1, we_right)
-        lag_block(right, 1, both_drain)

@@ -251,7 +251,7 @@ def tile_npchangetransitionprior_pa_kernel(tc, x, emb, Wg, bg, grad_out, out):
         grouped.append(regroup(first_units[1], shared))
         grouped.append(regroup(first_units[2], shared))
         quantise(first_units[1], grouped[1])
-        grouped.append(regroup(first_units[3], shared))
+        grouped.append(regroup(first_units[3], vector_only))
         quantise(first_units[2], grouped[2])
         quantise(first_units[3], grouped[3])
         diag_left = own_latent_products(0)

@@ -223,7 +223,7 @@ def tile_npchangetransitionprior_pa_kernel(tc, x, emb, Wg, bg, grad_out, out):
 
         make_identity(nc, identity[:])
         for part in range(PARTS):
-            nc.scalar.dma_start(
+            nc.sync.dma_start(
                 out=emb_raw[part:P:PARTS, :, :], in_=emb.rearrange("(c s) h -> s c h", c=PASSES)
             )
         load_g(0)

from contextlib import ExitStack

import concourse.mybir as mybir
from concourse.masks import make_identity

BF16 = mybir.dt.bfloat16
F32 = mybir.dt.float32
U32 = mybir.dt.uint32
U8 = mybir.dt.uint8
E4M3X4 = mybir.dt.float8_e4m3fn_x4
E5M2X4 = mybir.dt.float8_e5m2_x4

P = 128
B, T, D, H, L = 128, 10, 1024, 128, 2
TM = T - L
F = H + L * D + 1
PACK = 4
PASSES = B * TM // (P * PACK)
SERIES = B // PASSES
PARTS = P // SERIES
STEPS = PACK + L
HALF = 512
HALVES = D // HALF
M_TILES = D // P
M_PER_HALF = HALF // P
RUN = 4
ROW_PAD = 2056
GROUPED_BUFS = 4

FLOPS = 2 * B * TM * D * L * D + B * TM * D + 2 * B * D * H + 2 * B * TM * D
BYTES = 2 * (B * T * D + B * H + B * TM * D) + 4 * D * F


def tile_npchangetransitionprior_pa_kernel(tc, x, emb, Wg, bg, grad_out, out):
    nc = tc.nc
    mult = mybir.AluOpType.mult
    add = mybir.AluOpType.add

    with ExitStack() as ctx:
        keep = ctx.enter_context(tc.tile_pool(name="keep", bufs=1))
        stage = ctx.enter_context(tc.tile_pool(name="stage", bufs=GROUPED_BUFS))
        work = ctx.enter_context(tc.tile_pool(name="work", bufs=2))
        lag_banks = ctx.enter_context(tc.psum_pool(name="lag_banks", bufs=4))
        side_banks = ctx.enter_context(tc.psum_pool(name="side_banks", bufs=2))
        ctx.enter_context(tc.manual_schedule())

        g_raw = [keep.tile([P, PASSES, PACK, HALF], BF16, name="g_raw%d" % half) for half in range(HALVES)]
        x_raw = [
            [keep.tile([P, STEPS, HALF], BF16, name="x_raw%d_%d" % (c, half)) for half in range(HALVES)]
            for c in range(PASSES)
        ]
        emb_raw = keep.tile([P, PASSES, H], BF16)
        g_codes = keep.tile([P, PASSES, D], U32, align_bytes=64)
        g_scales = keep.tile([P, PASSES, D], U8, align_bytes=64)
        x_codes = keep.tile([P, L, PASSES, D], U32, align_bytes=64)
        x_scales = keep.tile([P, L, PASSES, D], U8, align_bytes=64)
        g_sum = keep.tile([P, PASSES, HALF], F32)
        emb_f32 = keep.tile([P, PASSES, H], F32)
        last_tokens = keep.tile([P, P], F32)
        identity = keep.tile([P, P], F32)
        lag_rows = keep.tile([P, M_TILES, ROW_PAD], F32)
        we_rows = keep.tile([P, M_TILES, H], F32)

        g_tokens = grad_out.rearrange("b t d -> (b t) d").rearrange(
            "(c p j) d -> c p j d", c=PASSES, p=P, j=PACK
        )

        def columns(half):
            return slice(half * HALF, (half + 1) * HALF)

        def load_g(half):
            for c in range(PASSES):
                nc.sync.dma_start(out=g_raw[half][:, c, :, :], in_=g_tokens[c, :, :, columns(half)])

        def load_x(half):
            for c in range(PASSES):
                for part in range(PARTS):
                    nc.sync.dma_start(
                        out=x_raw[c][half][part:P:PARTS, :, :],
                        in_=x[c * SERIES : (c + 1) * SERIES, part * PACK : part * PACK + STEPS, columns(half)],
                    )

        def g_unit(c, half):
            cols = columns(half)
            return (g_raw[half][:, c, :, :], g_codes[:, c, cols], g_scales[:, c, cols], E5M2X4)

        def x_unit(lag, c, half):
            cols = columns(half)
            return (
                x_raw[c][half][:, lag : lag + PACK, :],
                x_codes[:, lag, c, cols],
                x_scales[:, lag, c, cols],
                E4M3X4,
            )

        def regroup(unit, shares):
            grouped = stage.tile([P, HALF, PACK], BF16, align_bytes=64)
            for copy, share in shares:
                copy(
                    out=grouped[:, share, :].rearrange("p (w i) j -> p w j i", i=RUN),
                    in_=unit[0][:, :, share].rearrange("p j (w i) -> p w j i", i=RUN),
                )
            return grouped

        def quantise(unit, grouped):
            codes, scales, fmt = unit[1:]
            nc.vector.quantize_mx(
                out=codes.bitcast(fmt), scales=scales, in_=grouped[:].rearrange("p w j -> p (w j)")
            )

        def prepare(units, shares):
            grouped = [regroup(unit, shares) for unit in units]
            for unit, unit_grouped in zip(units, grouped):
                quantise(unit, unit_grouped)

        def lag_block(m_tiles, lag, half, drains):
            cols = columns(half)
            first = lag * D + half * HALF
            last = first + HALF + (1 if first + HALF == L * D else 0)
            for n, m in enumerate(m_tiles):
                d_cols = slice(m * P, (m + 1) * P)
                acc = lag_banks.tile([P, HALF], F32)
                for c in range(PASSES):
                    nc.tensor.matmul_mx(
                        out=acc[:],
                        lhsT=g_codes[:, c, d_cols].bitcast(E5M2X4),
                        lhsT_scale=g_scales[:, c, d_cols],
                        rhs=x_codes[:, lag, c, cols].bitcast(E4M3X4),
                        rhs_scale=x_scales[:, lag, c, cols],
                        start=(c == 0),
                        stop=(c == PASSES - 1),
                    )
                drains[n % len(drains)](out=lag_rows[:, m, first : first + HALF], in_=acc[:])
                nc.sync.dma_start(out=out[d_cols, H + first : H + last], in_=lag_rows[:, m, first:last])

        def own_latent_products(half):
            diag = side_banks.tile([P, M_PER_HALF, P], F32)
            for i in range(M_PER_HALF):
                for c in range(PASSES):
                    for j in range(PACK):
                        nc.tensor.matmul(
                            out=diag[:, i, :],
                            lhsT=g_raw[half][:, c, j, i * P : (i + 1) * P],
                            rhs=x_raw[c][half][:, j + L, i * P : (i + 1) * P],
                            start=(c == 0 and j == 0),
                            stop=(c == PASSES - 1 and j == PACK - 1),
                        )
            return diag

        def keep_diagonals(half, diag):
            masked = work.tile([P, M_PER_HALF, P], F32)
            nc.vector.tensor_tensor(
                out=masked[:],
                in0=diag[:],
                in1=identity[:].unsqueeze(1).to_broadcast([P, M_PER_HALF, P]),
                op=mult,
            )
            m_slots = slice(half * M_PER_HALF, (half + 1) * M_PER_HALF)
            nc.vector.tensor_reduce(
                out=lag_rows[:, m_slots, L * D], in_=masked[:], axis=mybir.AxisListType.X, op=add
            )

        def add_last_tokens(half):
            nc.vector.tensor_tensor(
                out=last_tokens[:],
                in0=g_raw[half][:, PASSES - 1, PACK - 2, HALF - P : HALF],
                in1=g_raw[half][:, PASSES - 1, PACK - 1, HALF - P : HALF],
                op=add,
            )

        def emb_products_by_token(half):
            d_we = side_banks.tile([P, M_PER_HALF, H], F32)
            slots = [(c, j) for c in range(PASSES) for j in range(PACK)]
            for i in range(M_PER_HALF):
                single = slots if i < M_PER_HALF - 1 else slots[:-2]
                for c, j in single:
                    nc.tensor.matmul(
                        out=d_we[:, i, :],
                        lhsT=g_raw[half][:, c, j, i * P : (i + 1) * P],
                        rhs=emb_raw[:, c, :],
                        start=((c, j) == slots[0]),
                        stop=((c, j) == slots[-1]),
                    )
            nc.tensor.matmul(
                out=d_we[:, M_PER_HALF - 1, :],
                lhsT=last_tokens[:],
                rhs=emb_f32[:, PASSES - 1, :],
                start=False,
                stop=True,
            )
            return d_we

        def sum_tokens(half):
            for c in range(PASSES):
                pair_sum = work.tile([P, 2, HALF], F32)
                nc.vector.tensor_tensor(
                    out=pair_sum[:], in0=g_raw[half][:, c, 0:2, :], in1=g_raw[half][:, c, 2:4, :], op=add
                )
                nc.vector.tensor_tensor(
                    out=g_sum[:, c, :], in0=pair_sum[:, 0, :], in1=pair_sum[:, 1, :], op=add
                )

        def emb_products_of_sums():
            d_we = side_banks.tile([P, M_PER_HALF, H], F32)
            for i in range(M_PER_HALF):
                for c in range(PASSES):
                    nc.tensor.matmul(
                        out=d_we[:, i, :],
                        lhsT=g_sum[:, c, i * P : (i + 1) * P],
                        rhs=emb_f32[:, c, :],
                        start=(c == 0),
                        stop=(c == PASSES - 1),
                    )
            return d_we

        def store_emb(half, d_we):
            m_slots = slice(half * M_PER_HALF, (half + 1) * M_PER_HALF)
            nc.scalar.copy(out=we_rows[:, m_slots, :], in_=d_we[:])
            nc.sync.dma_start(
                out=out[half * HALF : (half + 1) * HALF, 0:H].rearrange("(m p) h -> p m h", p=P),
                in_=we_rows[:, m_slots, :],
            )

        make_identity(nc, identity[:])
        for part in range(PARTS):
            nc.sync.dma_start(
                out=emb_raw[part:P:PARTS, :, :], in_=emb.rearrange("(c s) h -> s c h", c=PASSES)
            )
        load_g(0)
        load_x(0)
        load_g(1)
        load_x(1)

        left = range(M_PER_HALF)
        right = range(M_PER_HALF, M_TILES)
        shared = [(nc.vector.tensor_copy, slice(0, HALF // 2)), (nc.scalar.copy, slice(HALF // 2, HALF))]
        vector_only = [(nc.vector.tensor_copy, slice(0, HALF))]
        scalar_drains = [nc.scalar.copy]
        both_drain = [nc.scalar.copy, nc.vector.tensor_copy]

        left_units = [g_unit(c, 0) for c in range(PASSES)]
        left_grouped = [regroup(unit, shared) for unit in left_units]
        nc.vector.tensor_copy(out=emb_f32[:], in_=emb_raw[:])
        add_last_tokens(0)
        we_left = emb_products_by_token(0)
        for unit, unit_grouped in zip(left_units, left_grouped):
            quantise(unit, unit_grouped)
        first_units = [x_unit(lag, c, 0) for lag in range(L) for c in range(PASSES)]
        grouped = [regroup(first_units[0], shared)]
        quantise(first_units[0], grouped[0])
        grouped.append(regroup(first_units[1], shared))
        grouped.append(regroup(first_units[2], shared))
        quantise(first_units[1], grouped[1])
        grouped.append(regroup(first_units[3], vector_only))
        quantise(first_units[2], grouped[2])
        quantise(first_units[3], grouped[3])
        diag_left = own_latent_products(0)
        lag_block(left, 0, 0, scalar_drains)
        lag_block(left, 1, 0, scalar_drains)
        store_emb(0, we_left)
        prepare([g_unit(c, 1) for c in range(PASSES)], vector_only)
        diag_right = own_latent_products(1)
        lag_block(right, 0, 0, scalar_drains)
        lag_block(right, 1, 0, scalar_drains)
        for lag in range(L):
            prepare([x_unit(lag, c, 1) for c in range(PASSES)], vector_only)
        keep_diagonals(0, diag_left)
        keep_diagonals(1, diag_right)
        lag_block(left, 0, 1, scalar_drains)
        lag_block(right, 0, 1, scalar_drains)
        sum_tokens(1)
        lag_block(left, 1, 1, scalar_drains)
        lag_block(right, 1, 1, both_drain)
        we_right = emb_products_of_sums()
        store_emb(1, we_right)
